import numpy as np
import ml_dtypes


def mxq(x, axis, fmt="e4m3"):
    dtype, down = {"e4m3": (ml_dtypes.float8_e4m3fn, 7), "e5m2": (ml_dtypes.float8_e5m2, 14)}[fmt]
    v = np.moveaxis(np.asarray(x, np.float32).astype(ml_dtypes.bfloat16).astype(np.float64), axis, -1)
    blocks = v.reshape(v.shape[:-1] + (-1, 32))
    amax = np.abs(blocks).max(-1, keepdims=True)
    byte = np.maximum(np.where(amax > 0, np.frexp(amax)[1] - 1 + 127, 0) - down, 1)
    scale = np.exp2(byte - 127.0)
    codes = (blocks / scale).astype(np.float32).astype(dtype).astype(np.float64)
    return np.moveaxis((codes * scale).reshape(v.shape), -1, axis)


WIDE = False


def mx_kscale(k):
    if not WIDE:
        return np.ones(k)
    levels = np.array([10, -10, 5, -5, 0])
    a = np.random.permutation(np.resize(levels, k // 512 * 4)).reshape(k // 512, 4)
    idx = np.arange(k)
    return np.exp2(a[idx // 512, idx % 128 // 32])


BF16 = ml_dtypes.bfloat16


def bf(x):
    return np.asarray(x, np.float32).astype(BF16)


def f64(x):
    return np.asarray(x).astype(np.float64)


BATCH, IN_DIM, OUT_DIM = 16384, 512, 256


def setup_inputs():
    s = mx_kscale(IN_DIM)
    a = np.round(np.log2(s))
    x = np.random.standard_normal((BATCH, IN_DIM)) * (8.0 / np.sqrt(IN_DIM)) * s
    shift = np.round(np.random.uniform(-10.0, -1.0, (IN_DIM, OUT_DIM))) - a[:, None]
    sign = np.round(np.random.uniform(0.0, 1.0, (IN_DIM, OUT_DIM)))
    bias = np.random.standard_normal((1, OUT_DIM)) * 0.5
    return {"x": bf(x), "shift": bf(shift), "sign": bf(sign), "bias": bf(bias)}


def reference(x, shift, sign, bias):
    W = np.exp2(f64(shift)) * np.power(-1.0, f64(sign))
    return (mxq(f64(x), 1, "e4m3") @ mxq(W, 0, "e4m3")) + f64(bias)

@@ -1,0 +1,177 @@
+from contextlib import ExitStack
+
+import concourse.masks as masks
+import concourse.mybir as mybir
+
+FLOPS = 2 * 16384 * 512 * 256
+
+F32 = mybir.dt.float32
+BF16 = mybir.dt.bfloat16
+I32 = mybir.dt.int32
+U32 = mybir.dt.uint32
+U8 = mybir.dt.uint8
+FP8X4 = mybir.dt.float8_e4m3fn_x4
+ALU = mybir.AluOpType
+ACTF = mybir.ActivationFunctionType
+
+P = 128
+ROWS = 16384
+K = 512
+N = 256
+KW = K // 2
+T_ALL = ROWS // P
+UNIT = 4
+NU = T_ALL // UNIT
+
+X_CHUNKS = [1, 1, 2, 4, 4, 4, 4, 4, 4, 4]
+O_CHUNKS = [4, 4, 4, 4, 4, 4, 4, 2, 2]
+LOADS_AHEAD = 7
+
+
+def tile_denseshift_kernel(tc, x, shift, sign, bias, out):
+    nc = tc.nc
+    xv = x.rearrange("(p t) k -> p (t k)", t=T_ALL)
+    ov = out.rearrange("(p t) n -> p (t n)", t=T_ALL)
+
+    with ExitStack() as ctx:
+        const = ctx.enter_context(tc.tile_pool(name="const", bufs=1))
+        wp = ctx.enter_context(tc.tile_pool(name="wp", bufs=1))
+        xs_pool = ctx.enter_context(tc.tile_pool(name="xs", bufs=1))
+        xb_pool = ctx.enter_context(tc.tile_pool(name="xb", bufs=6))
+        o_pool = ctx.enter_context(tc.tile_pool(name="o", bufs=4))
+        g_pool = ctx.enter_context(tc.tile_pool(name="g", bufs=4))
+        c_pool = ctx.enter_context(tc.tile_pool(name="c", bufs=3))
+        ps_t = ctx.enter_context(tc.psum_pool(name="pst", bufs=4))
+        ps_a = ctx.enter_context(tc.psum_pool(name="psa", bufs=4))
+        ctx.enter_context(tc.manual_schedule())
+
+        unit_src = {}
+        x_start = [sum(X_CHUNKS[:c]) for c in range(len(X_CHUNKS))]
+
+        def load(c):
+            n = X_CHUNKS[c]
+            u0 = x_start[c]
+            if n < 4:
+                xt = xs_pool.tile([P, n * UNIT * K], BF16, name="xs%d" % c)
+            else:
+                xt = xb_pool.tile([P, n * UNIT * K], BF16, name="xb", tag="xb")
+            nc.sync.dma_start(out=xt[:], in_=xv[:, u0 * UNIT * K:(u0 + n) * UNIT * K])
+            for i in range(n):
+                unit_src[u0 + i] = (xt, i)
+
+        sh = wp.tile([P, 4 * N], BF16)
+        sn = wp.tile([P, 4 * N], BF16)
+        nc.scalar.dma_start(out=sh[:].rearrange("p (u f) -> p u f", u=2),
+                            in_=shift.rearrange("(u q e) c -> q u (e c)", u=2, e=2))
+        nc.scalar.dma_start(out=sn[:].rearrange("p (u f) -> p u f", u=2),
+                            in_=sign.rearrange("(u q e) c -> q u (e c)", u=2, e=2))
+        for c in range(LOADS_AHEAD):
+            load(c)
+
+        ident = const.tile([P, P], F32)
+        masks.make_identity(nc, ident[:])
+        ones = const.tile([P, P], BF16)
+        nc.vector.memset(ones[:], 1.0)
+        brow = const.tile([P, N], BF16)
+        nc.vector.memset(brow[:], 0.0)
+        nc.scalar.dma_start(out=brow[0:1, :], in_=bias)
+
+        ef = wp.tile([P, 4 * N], F32)
+        nc.vector.tensor_scalar(out=ef[:], in0=sh[:], scalar1=float(2 ** 23), scalar2=float(127 * 2 ** 23),
+                                op0=ALU.mult, op1=ALU.add)
+        eb = wp.tile([P, 4 * N], I32)
+        nc.vector.tensor_scalar(out=eb[:], in0=ef[:], scalar1=0.0, scalar2=float(255 * 2 ** 23),
+                                op0=ALU.max, op1=ALU.min)
+        sg = wp.tile([P, 4 * N], F32)
+        nc.scalar.activation(out=sg[:], in_=sn[:], func=ACTF.Copy, bias=1.0, scale=-2.0)
+        wg = wp.tile([P, 4 * N], BF16, align_bytes=64)
+        nc.vector.tensor_tensor(out=wg[:].rearrange("p (c t) -> p c t", t=4),
+                                in0=eb[:].bitcast(F32).rearrange("p (t c) -> p c t", t=4),
+                                in1=sg[:].rearrange("p (t c) -> p c t", t=4), op=ALU.mult)
+        wc = wp.tile([P, N], U32, align_bytes=64)
+        ws = wp.tile([P, N], U8, align_bytes=64)
+        nc.vector.quantize_mx(out=wc[:].bitcast(FP8X4), scales=ws[:], in_=wg[:])
+
+        bias2 = const.tile([P, 2 * N], F32)
+
+        def transposes(u):
+            xt, lu = unit_src[u]
+            xw = xt[:].bitcast(F32)
+            banks = []
+            for b in range(2):
+                tp = ps_t.tile([P, 512], F32, name="tp", tag="tp")
+                for j in range(2):
+                    for h in range(2):
+                        col = ((lu * UNIT + 2 * b + j) * 2 + h) * P
+                        nc.tensor.transpose(tp[:, (2 * j + h) * P:(2 * j + h + 1) * P], xw[:, col:col + P], ident[:])
+                banks.append(tp)
+            return banks
+
+        def copy_out(banks):
+            g = g_pool.tile([P, UNIT * K], BF16, name="g", tag="g", align_bytes=64)
+            g32 = g[:].bitcast(F32)
+            for b in range(2):
+                nc.scalar.copy(out=g32[:, b * 512:(b + 1) * 512].rearrange("p (j r h) -> p j r h", j=2, h=2),
+                               in_=banks[b][:].rearrange("p (j h r) -> p j r h", j=2, h=2))
+            return g
+
+        def quantise(g):
+            cw = c_pool.tile([P, UNIT * P], U32, name="cw", tag="cw", align_bytes=64)
+            cs = c_pool.tile([P, UNIT * P], U8, name="cs", tag="cs", align_bytes=64)
+            nc.vector.quantize_mx(out=cw[:].bitcast(FP8X4), scales=cs[:], in_=g[:])
+            return (cw, cs)
+
+        def passes(q):
+            cw, cs = q
+            accs = []
+            for b in range(2):
+                acc = ps_a.tile([P, 2 * N], F32, name="acc", tag="acc")
+                for j in range(2):
+                    m = (2 * b + j) * P
+                    nc.tensor.matmul_mx(out=acc[:, j * N:(j + 1) * N],
+                                        lhsT=cw[:, m:m + P].bitcast(FP8X4), lhsT_scale=cs[:, m:m + P],
+                                        rhs=wc[:].bitcast(FP8X4), rhs_scale=ws[:], start=True, stop=True)
+                accs.append(acc)
+            return accs
+
+        o_start = [sum(O_CHUNKS[:c]) for c in range(len(O_CHUNKS))]
+        o_of_unit = {}
+        for c in range(len(O_CHUNKS)):
+            for i in range(O_CHUNKS[c]):
+                o_of_unit[o_start[c] + i] = (c, i)
+        o_tiles = {}
+        state = {"next_load": LOADS_AHEAD}
+
+        def add_bias(u, accs):
+            c, i = o_of_unit[u]
+            if i == 0:
+                o_tiles[c] = o_pool.tile([P, O_CHUNKS[c] * UNIT * N], F32, name="o", tag="o")
+            ot = o_tiles[c]
+            for b in range(2):
+                col = (i * UNIT + 2 * b) * N
+                nc.vector.tensor_tensor(out=ot[:, col:col + 2 * N], in0=accs[b][:], in1=bias2[:], op=ALU.add)
+            if i == O_CHUNKS[c] - 1:
+                u0 = o_start[c]
+                nc.sync.dma_start(out=ov[:, u0 * UNIT * N:(u + 1) * UNIT * N], in_=ot[:])
+                if state["next_load"] < len(X_CHUNKS):
+                    load(state["next_load"])
+                    state["next_load"] = state["next_load"] + 1
+
+        gs = {}
+        qs = {}
+        for j in range(NU + 2):
+            if j < NU:
+                gs[j] = copy_out(transposes(j))
+            if j == 1:
+                pb = ps_a.tile([P, 2 * N], F32, name="acc", tag="acc")
+                for i in range(2):
+                    nc.tensor.matmul(pb[:, i * N:(i + 1) * N], lhsT=ones[:], rhs=brow[:], start=True, stop=True)
+            accs = None
+            if j >= 2:
+                accs = passes(qs[j - 2])
+            if 1 <= j <= NU:
+                qs[j - 1] = quantise(gs[j - 1])
+            if j == 1:
+                nc.vector.tensor_copy(out=bias2[:], in_=pb[:])
+            if j >= 2:
+                add_bias(j - 2, accs)

@@ -23,9 +23,9 @@ T_ALL = ROWS // P
 UNIT = 4
 NU = T_ALL // UNIT
 
-X_CHUNKS = [1, 1, 2, 4, 4, 4, 4, 4, 4, 4]
-O_CHUNKS = [4, 4, 4, 4, 4, 4, 4, 2, 2]
-LOADS_AHEAD = 7
+X_TILE = 4
+X_PIECES = {0: [1, 1, 2], 1: [2, 2]}
+O_CHUNKS = [4, 4, 4, 4, 4, 4, 4, 2, 1, 1]
 
 
 def tile_denseshift_kernel(tc, x, shift, sign, bias, out):
@@ -36,9 +36,7 @@ def tile_denseshift_kernel(tc, x, shift, sign, bias, out):
     with ExitStack() as ctx:
         const = ctx.enter_context(tc.tile_pool(name="const", bufs=1))
         wp = ctx.enter_context(tc.tile_pool(name="wp", bufs=1))
-        xs_pool = ctx.enter_context(tc.tile_pool(name="xs", bufs=1))
-        xb_pool = ctx.enter_context(tc.tile_pool(name="xb", bufs=6))
-        o_pool = ctx.enter_context(tc.tile_pool(name="o", bufs=4))
+        m_pool = ctx.enter_context(tc.tile_pool(name="m", bufs=11))
         g_pool = ctx.enter_context(tc.tile_pool(name="g", bufs=4))
         c_pool = ctx.enter_context(tc.tile_pool(name="c", bufs=3))
         ps_t = ctx.enter_context(tc.psum_pool(name="pst", bufs=4))
@@ -46,35 +44,34 @@ def tile_denseshift_kernel(tc, x, shift, sign, bias, out):
         ctx.enter_context(tc.manual_schedule())
 
         unit_src = {}
-        x_start = [sum(X_CHUNKS[:c]) for c in range(len(X_CHUNKS))]
 
         def load(c):
-            n = X_CHUNKS[c]
-            u0 = x_start[c]
-            if n < 4:
-                xt = xs_pool.tile([P, n * UNIT * K], BF16, name="xs%d" % c)
-            else:
-                xt = xb_pool.tile([P, n * UNIT * K], BF16, name="xb", tag="xb")
-            nc.sync.dma_start(out=xt[:], in_=xv[:, u0 * UNIT * K:(u0 + n) * UNIT * K])
-            for i in range(n):
-                unit_src[u0 + i] = (xt, i)
+            xt = m_pool.tile([P, X_TILE * UNIT * K], BF16, name="xt", tag="m")
+            a = 0
+            for n in X_PIECES.get(c, [X_TILE]):
+                u0 = c * X_TILE + a
+                nc.sync.dma_start(out=xt[:, a * UNIT * K:(a + n) * UNIT * K],
+                                  in_=xv[:, u0 * UNIT * K:(u0 + n) * UNIT * K])
+                a += n
+            for i in range(X_TILE):
+                unit_src[c * X_TILE + i] = (xt, i)
 
         sh = wp.tile([P, 4 * N], BF16)
         sn = wp.tile([P, 4 * N], BF16)
-        nc.scalar.dma_start(out=sh[:].rearrange("p (u f) -> p u f", u=2),
-                            in_=shift.rearrange("(u q e) c -> q u (e c)", u=2, e=2))
-        nc.scalar.dma_start(out=sn[:].rearrange("p (u f) -> p u f", u=2),
-                            in_=sign.rearrange("(u q e) c -> q u (e c)", u=2, e=2))
-        for c in range(LOADS_AHEAD):
+        nc.sync.dma_start(out=sh[:].rearrange("p (u f) -> p u f", u=2),
+                          in_=shift.rearrange("(u q e) c -> q u (e c)", u=2, e=2))
+        nc.sync.dma_start(out=sn[:].rearrange("p (u f) -> p u f", u=2),
+                          in_=sign.rearrange("(u q e) c -> q u (e c)", u=2, e=2))
+        brow = const.tile([P, N], BF16)
+        nc.vector.memset(brow[:], 0.0)
+        nc.sync.dma_start(out=brow[0:1, :], in_=bias)
+        for c in range(NU // X_TILE):
             load(c)
 
         ident = const.tile([P, P], F32)
         masks.make_identity(nc, ident[:])
         ones = const.tile([P, P], BF16)
         nc.vector.memset(ones[:], 1.0)
-        brow = const.tile([P, N], BF16)
-        nc.vector.memset(brow[:], 0.0)
-        nc.scalar.dma_start(out=brow[0:1, :], in_=bias)
 
         ef = wp.tile([P, 4 * N], F32)
         nc.vector.tensor_scalar(out=ef[:], in0=sh[:], scalar1=float(2 ** 23), scalar2=float(127 * 2 ** 23),
@@ -140,12 +137,11 @@ def tile_denseshift_kernel(tc, x, shift, sign, bias, out):
             for i in range(O_CHUNKS[c]):
                 o_of_unit[o_start[c] + i] = (c, i)
         o_tiles = {}
-        state = {"next_load": LOADS_AHEAD}
 
         def add_bias(u, accs):
             c, i = o_of_unit[u]
             if i == 0:
-                o_tiles[c] = o_pool.tile([P, O_CHUNKS[c] * UNIT * N], F32, name="o", tag="o")
+                o_tiles[c] = m_pool.tile([P, O_CHUNKS[c] * UNIT * N], F32, name="ot", tag="m")
             ot = o_tiles[c]
             for b in range(2):
                 col = (i * UNIT + 2 * b) * N
@@ -153,9 +149,6 @@ def tile_denseshift_kernel(tc, x, shift, sign, bias, out):
             if i == O_CHUNKS[c] - 1:
                 u0 = o_start[c]
                 nc.sync.dma_start(out=ov[:, u0 * UNIT * N:(u + 1) * UNIT * N], in_=ot[:])
-                if state["next_load"] < len(X_CHUNKS):
-                    load(state["next_load"])
-                    state["next_load"] = state["next_load"] + 1
 
         gs = {}
         qs = {}

@@ -23,9 +23,9 @@ T_ALL = ROWS // P
 UNIT = 4
 NU = T_ALL // UNIT
 
-X_TILE = 4
-X_PIECES = {0: [1, 1, 2], 1: [2, 2]}
-O_CHUNKS = [4, 4, 4, 4, 4, 4, 4, 2, 1, 1]
+UB = UNIT * K * 2
+X_TILES = [(0, 4, 1, [1, 1, 2]), (4, 3, 5, [3]), (7, 5, 8, [5]), (12, 8, 13, [8]), (20, 12, 21, [12])]
+O_TILES = [(0, 8, 33), (8, 8, 0), (16, 5, 8), (21, 3, 13), (24, 3, 16), (27, 3, 33), (30, 2, 36)]
 
 
 def tile_denseshift_kernel(tc, x, shift, sign, bias, out):
@@ -36,7 +36,7 @@ def tile_denseshift_kernel(tc, x, shift, sign, bias, out):
     with ExitStack() as ctx:
         const = ctx.enter_context(tc.tile_pool(name="const", bufs=1))
         wp = ctx.enter_context(tc.tile_pool(name="wp", bufs=1))
-        m_pool = ctx.enter_context(tc.tile_pool(name="m", bufs=11))
+        m_pool = ctx.enter_context(tc.tile_pool(name="m", bufs=1))
         g_pool = ctx.enter_context(tc.tile_pool(name="g", bufs=4))
         c_pool = ctx.enter_context(tc.tile_pool(name="c", bufs=3))
         ps_t = ctx.enter_context(tc.psum_pool(name="pst", bufs=4))
@@ -46,15 +46,16 @@ def tile_denseshift_kernel(tc, x, shift, sign, bias, out):
         unit_src = {}
 
         def load(c):
-            xt = m_pool.tile([P, X_TILE * UNIT * K], BF16, name="xt", tag="m")
+            first, units, place, pieces = X_TILES[c]
+            xt = m_pool.tile([P, units * UNIT * K], BF16, name="xt%d" % c, offset=place * UB)
             a = 0
-            for n in X_PIECES.get(c, [X_TILE]):
-                u0 = c * X_TILE + a
+            for n in pieces:
+                u0 = first + a
                 nc.sync.dma_start(out=xt[:, a * UNIT * K:(a + n) * UNIT * K],
                                   in_=xv[:, u0 * UNIT * K:(u0 + n) * UNIT * K])
                 a += n
-            for i in range(X_TILE):
-                unit_src[c * X_TILE + i] = (xt, i)
+            for i in range(units):
+                unit_src[first + i] = (xt, i)
 
         sh = wp.tile([P, 4 * N], BF16)
         sn = wp.tile([P, 4 * N], BF16)
@@ -65,7 +66,7 @@ def tile_denseshift_kernel(tc, x, shift, sign, bias, out):
         brow = const.tile([P, N], BF16)
         nc.vector.memset(brow[:], 0.0)
         nc.sync.dma_start(out=brow[0:1, :], in_=bias)
-        for c in range(NU // X_TILE):
+        for c in range(len(X_TILES)):
             load(c)
 
         ident = const.tile([P, P], F32)
@@ -131,24 +132,23 @@ def tile_denseshift_kernel(tc, x, shift, sign, bias, out):
                 accs.append(acc)
             return accs
 
-        o_start = [sum(O_CHUNKS[:c]) for c in range(len(O_CHUNKS))]
         o_of_unit = {}
-        for c in range(len(O_CHUNKS)):
-            for i in range(O_CHUNKS[c]):
-                o_of_unit[o_start[c] + i] = (c, i)
+        for c in range(len(O_TILES)):
+            for i in range(O_TILES[c][1]):
+                o_of_unit[O_TILES[c][0] + i] = (c, i)
         o_tiles = {}
 
         def add_bias(u, accs):
             c, i = o_of_unit[u]
+            first, units, place = O_TILES[c]
             if i == 0:
-                o_tiles[c] = m_pool.tile([P, O_CHUNKS[c] * UNIT * N], F32, name="ot", tag="m")
+                o_tiles[c] = m_pool.tile([P, units * UNIT * N], F32, name="ot%d" % c, offset=place * UB)
             ot = o_tiles[c]
             for b in range(2):
                 col = (i * UNIT + 2 * b) * N
                 nc.vector.tensor_tensor(out=ot[:, col:col + 2 * N], in0=accs[b][:], in1=bias2[:], op=ALU.add)
-            if i == O_CHUNKS[c] - 1:
-                u0 = o_start[c]
-                nc.sync.dma_start(out=ov[:, u0 * UNIT * N:(u + 1) * UNIT * N], in_=ot[:])
+            if i == units - 1:
+                nc.sync.dma_start(out=ov[:, first * UNIT * N:(u + 1) * UNIT * N], in_=ot[:])
 
         gs = {}
         qs = {}

@@ -12,7 +12,6 @@ U32 = mybir.dt.uint32
 U8 = mybir.dt.uint8
 FP8X4 = mybir.dt.float8_e4m3fn_x4
 ALU = mybir.AluOpType
-ACTF = mybir.ActivationFunctionType
 
 P = 128
 ROWS = 16384
@@ -81,7 +80,7 @@ def tile_denseshift_kernel(tc, x, shift, sign, bias, out):
         nc.vector.tensor_scalar(out=eb[:], in0=ef[:], scalar1=0.0, scalar2=float(255 * 2 ** 23),
                                 op0=ALU.max, op1=ALU.min)
         sg = wp.tile([P, 4 * N], F32)
-        nc.scalar.activation(out=sg[:], in_=sn[:], func=ACTF.Copy, bias=1.0, scale=-2.0)
+        nc.vector.tensor_scalar(out=sg[:], in0=sn[:], scalar1=-2.0, scalar2=1.0, op0=ALU.mult, op1=ALU.add)
         wg = wp.tile([P, 4 * N], BF16, align_bytes=64)
         nc.vector.tensor_tensor(out=wg[:].rearrange("p (c t) -> p c t", t=4),
                                 in0=eb[:].bitcast(F32).rearrange("p (t c) -> p c t", t=4),

from contextlib import ExitStack

import concourse.masks as masks
import concourse.mybir as mybir

FLOPS = 2 * 16384 * 512 * 256

F32 = mybir.dt.float32
BF16 = mybir.dt.bfloat16
I32 = mybir.dt.int32
U32 = mybir.dt.uint32
U8 = mybir.dt.uint8
FP8X4 = mybir.dt.float8_e4m3fn_x4
ALU = mybir.AluOpType

P = 128
ROWS = 16384
K = 512
N = 256
KW = K // 2
T_ALL = ROWS // P
UNIT = 4
NU = T_ALL // UNIT

UB = UNIT * K * 2
X_TILES = [(0, 4, 1, [1, 1, 2]), (4, 3, 5, [3]), (7, 5, 8, [5]), (12, 8, 13, [8]), (20, 12, 21, [12])]
O_TILES = [(0, 8, 33), (8, 8, 0), (16, 5, 8), (21, 3, 13), (24, 3, 16), (27, 3, 33), (30, 2, 36)]


def tile_denseshift_kernel(tc, x, shift, sign, bias, out):
    nc = tc.nc
    xv = x.rearrange("(p t) k -> p (t k)", t=T_ALL)
    ov = out.rearrange("(p t) n -> p (t n)", t=T_ALL)

    with ExitStack() as ctx:
        const = ctx.enter_context(tc.tile_pool(name="const", bufs=1))
        wp = ctx.enter_context(tc.tile_pool(name="wp", bufs=1))
        m_pool = ctx.enter_context(tc.tile_pool(name="m", bufs=1))
        g_pool = ctx.enter_context(tc.tile_pool(name="g", bufs=4))
        c_pool = ctx.enter_context(tc.tile_pool(name="c", bufs=3))
        ps_t = ctx.enter_context(tc.psum_pool(name="pst", bufs=4))
        ps_a = ctx.enter_context(tc.psum_pool(name="psa", bufs=4))
        ctx.enter_context(tc.manual_schedule())

        unit_src = {}

        def load(c):
            first, units, place, pieces = X_TILES[c]
            xt = m_pool.tile([P, units * UNIT * K], BF16, name="xt%d" % c, offset=place * UB)
            a = 0
            for n in pieces:
                u0 = first + a
                nc.sync.dma_start(out=xt[:, a * UNIT * K:(a + n) * UNIT * K],
                                  in_=xv[:, u0 * UNIT * K:(u0 + n) * UNIT * K])
                a += n
            for i in range(units):
                unit_src[first + i] = (xt, i)

        sh = wp.tile([P, 4 * N], BF16)
        sn = wp.tile([P, 4 * N], BF16)
        nc.sync.dma_start(out=sh[:].rearrange("p (u f) -> p u f", u=2),
                          in_=shift.rearrange("(u q e) c -> q u (e c)", u=2, e=2))
        nc.sync.dma_start(out=sn[:].rearrange("p (u f) -> p u f", u=2),
                          in_=sign.rearrange("(u q e) c -> q u (e c)", u=2, e=2))
        brow = const.tile([P, N], BF16)
        nc.vector.memset(brow[:], 0.0)
        nc.sync.dma_start(out=brow[0:1, :], in_=bias)
        for c in range(len(X_TILES)):
            load(c)

        ident = const.tile([P, P], F32)
        masks.make_identity(nc, ident[:])
        ones = const.tile([P, P], BF16)
        nc.vector.memset(ones[:], 1.0)

        ef = wp.tile([P, 4 * N], F32)
        nc.vector.tensor_scalar(out=ef[:], in0=sh[:], scalar1=float(2 ** 23), scalar2=float(127 * 2 ** 23),
                                op0=ALU.mult, op1=ALU.add)
        eb = wp.tile([P, 4 * N], I32)
        nc.vector.tensor_scalar(out=eb[:], in0=ef[:], scalar1=0.0, scalar2=float(255 * 2 ** 23),
                                op0=ALU.max, op1=ALU.min)
        sg = wp.tile([P, 4 * N], F32)
        nc.vector.tensor_scalar(out=sg[:], in0=sn[:], scalar1=-2.0, scalar2=1.0, op0=ALU.mult, op1=ALU.add)
        wg = wp.tile([P, 4 * N], BF16, align_bytes=64)
        nc.vector.tensor_tensor(out=wg[:].rearrange("p (c t) -> p c t", t=4),
                                in0=eb[:].bitcast(F32).rearrange("p (t c) -> p c t", t=4),
                                in1=sg[:].rearrange("p (t c) -> p c t", t=4), op=ALU.mult)
        wc = wp.tile([P, N], U32, align_bytes=64)
        ws = wp.tile([P, N], U8, align_bytes=64)
        nc.vector.quantize_mx(out=wc[:].bitcast(FP8X4), scales=ws[:], in_=wg[:])

        bias2 = const.tile([P, 2 * N], F32)

        def transposes(u):
            xt, lu = unit_src[u]
            xw = xt[:].bitcast(F32)
            banks = []
            for b in range(2):
                tp = ps_t.tile([P, 512], F32, name="tp", tag="tp")
                for j in range(2):
                    for h in range(2):
                        col = ((lu * UNIT + 2 * b + j) * 2 + h) * P
                        nc.tensor.transpose(tp[:, (2 * j + h) * P:(2 * j + h + 1) * P], xw[:, col:col + P], ident[:])
                banks.append(tp)
            return banks

        def copy_out(banks):
            g = g_pool.tile([P, UNIT * K], BF16, name="g", tag="g", align_bytes=64)
            g32 = g[:].bitcast(F32)
            for b in range(2):
                nc.scalar.copy(out=g32[:, b * 512:(b + 1) * 512].rearrange("p (j r h) -> p j r h", j=2, h=2),
                               in_=banks[b][:].rearrange("p (j h r) -> p j r h", j=2, h=2))
            return g

        def quantise(g):
            cw = c_pool.tile([P, UNIT * P], U32, name="cw", tag="cw", align_bytes=64)
            cs = c_pool.tile([P, UNIT * P], U8, name="cs", tag="cs", align_bytes=64)
            nc.vector.quantize_mx(out=cw[:].bitcast(FP8X4), scales=cs[:], in_=g[:])
            return (cw, cs)

        def passes(q):
            cw, cs = q
            accs = []
            for b in range(2):
                acc = ps_a.tile([P, 2 * N], F32, name="acc", tag="acc")
                for j in range(2):
                    m = (2 * b + j) * P
                    nc.tensor.matmul_mx(out=acc[:, j * N:(j + 1) * N],
                                        lhsT=cw[:, m:m + P].bitcast(FP8X4), lhsT_scale=cs[:, m:m + P],
                                        rhs=wc[:].bitcast(FP8X4), rhs_scale=ws[:], start=True, stop=True)
                accs.append(acc)
            return accs

        o_of_unit = {}
        for c in range(len(O_TILES)):
            for i in range(O_TILES[c][1]):
                o_of_unit[O_TILES[c][0] + i] = (c, i)
        o_tiles = {}

        def add_bias(u, accs):
            c, i = o_of_unit[u]
            first, units, place = O_TILES[c]
            if i == 0:
                o_tiles[c] = m_pool.tile([P, units * UNIT * N], F32, name="ot%d" % c, offset=place * UB)
            ot = o_tiles[c]
            for b in range(2):
                col = (i * UNIT + 2 * b) * N
                nc.vector.tensor_tensor(out=ot[:, col:col + 2 * N], in0=accs[b][:], in1=bias2[:], op=ALU.add)
            if i == units - 1:
                nc.sync.dma_start(out=ov[:, first * UNIT * N:(u + 1) * UNIT * N], in_=ot[:])

        gs = {}
        qs = {}
        for j in range(NU + 2):
            if j < NU:
                gs[j] = copy_out(transposes(j))
            if j == 1:
                pb = ps_a.tile([P, 2 * N], F32, name="acc", tag="acc")
                for i in range(2):
                    nc.tensor.matmul(pb[:, i * N:(i + 1) * N], lhsT=ones[:], rhs=brow[:], start=True, stop=True)
            accs = None
            if j >= 2:
                accs = passes(qs[j - 2])
            if 1 <= j <= NU:
                qs[j - 1] = quantise(gs[j - 1])
            if j == 1:
                nc.vector.tensor_copy(out=bias2[:], in_=pb[:])
            if j >= 2:
                add_bias(j - 2, accs)
